import numpy as np
import ml_dtypes

BF16 = ml_dtypes.bfloat16


def bf(x):
    return np.asarray(x, np.float32).astype(BF16)


def f32(x):
    return np.asarray(x, np.float32)


def f64(x):
    return np.asarray(x).astype(np.float64)


def striped(idx):
    return np.tile(idx.reshape(-1, 16).T, (8, 1))


S, D, M, N = 1024, 128, 256, 2048


def setup_inputs():
    return {"table": bf(np.random.standard_normal((D, S))), "w": bf(np.random.standard_normal((D, M)) / np.sqrt(D)), "offs": striped(np.random.permutation(np.tile(np.arange(S), 2))[:N])}


def reference(table, w, offs):
    idx = offs[:16].T.reshape(-1)
    z = f64(w).T @ f64(table)[:, idx]
    return z - np.log(np.exp(z).sum(axis=1, keepdims=True))

@@ -1,0 +1,68 @@
+import concourse.mybir as mybir
+
+BF16, F32, U16 = mybir.dt.bfloat16, mybir.dt.float32, mybir.dt.uint16
+ALU = mybir.AluOpType
+ACT = mybir.ActivationFunctionType
+FREE_AXIS = mybir.AxisListType.X
+
+P = 128
+WORDS = 1024
+TOKENS = 2048
+BLOCKS = 2
+PIECE = 512
+PIECES = TOKENS // PIECE
+PIECE_OFFSET_COLS = PIECE // 16
+
+FLOPS = 2 * P * BLOCKS * P * TOKENS
+
+
+def tile_word2vec_kernel(tc, table, w, offs, out):
+    nc = tc.nc
+    with (
+        tc.tile_pool(name="held", bufs=1) as held,
+        tc.tile_pool(name="scratch", bufs=2) as scratch,
+        tc.tile_pool(name="staging", bufs=4) as staging,
+        tc.psum_pool(name="psum", bufs=1) as psum,
+    ):
+        offsets = held.tile([P, TOKENS // 16], U16, name="offsets")
+        nc.sync.dma_start(offsets[:], offs)
+        table_sb = held.tile([P, WORDS], BF16, name="table_sb")
+        nc.scalar.dma_start(table_sb[:], table)
+        w_sb = held.tile([P, BLOCKS * P], BF16, name="w_sb")
+        nc.sync.dma_start(w_sb[:], w)
+
+        for b in range(BLOCKS):
+            z = [psum.tile([P, PIECE], F32, name=f"z_{b}_{p}") for p in range(PIECES)]
+            piece_max = held.tile([P, PIECES], F32, name=f"piece_max_{b}")
+            for p in range(PIECES):
+                piece_offsets = offsets[:, p * PIECE_OFFSET_COLS : (p + 1) * PIECE_OFFSET_COLS]
+                nc.tensor.matmul(
+                    z[p][:],
+                    w_sb[:, b * P : (b + 1) * P],
+                    table_sb[:].indirect(piece_offsets),
+                    start=True,
+                    stop=True,
+                )
+                nc.vector.reduce_max(piece_max[:, p : p + 1], z[p][:], axis=FREE_AXIS)
+
+            neg_max = held.tile([P, 1], F32, name=f"neg_max_{b}")
+            nc.vector.tensor_reduce(neg_max[:], piece_max[:], axis=FREE_AXIS, op=ALU.max, negate=True)
+
+            piece_sum = held.tile([P, PIECES], F32, name=f"piece_sum_{b}")
+            for p in range(PIECES):
+                exp_unused = scratch.tile([P, PIECE], F32, name="exp_unused")
+                nc.scalar.activation(
+                    exp_unused[:], z[p][:], ACT.Exp, bias=neg_max[:], scale=1.0,
+                    accum_out=piece_sum[:, p : p + 1],
+                )
+            exp_sum = held.tile([P, 1], F32, name=f"exp_sum_{b}")
+            nc.vector.reduce_sum(exp_sum[:], piece_sum[:], axis=FREE_AXIS)
+            log_sum = held.tile([P, 1], F32, name=f"log_sum_{b}")
+            nc.scalar.activation(log_sum[:], exp_sum[:], ACT.Ln)
+
+            for p in range(PIECES):
+                result = staging.tile([P, PIECE], F32, name="result")
+                nc.vector.tensor_scalar(
+                    result[:], z[p][:], neg_max[:], log_sum[:], op0=ALU.add, op1=ALU.subtract
+                )
+                nc.sync.dma_start(out[b * P : (b + 1) * P, p * PIECE : (p + 1) * PIECE], result[:])

@@ -21,7 +21,7 @@ def tile_word2vec_kernel(tc, table, w, offs, out):
     with (
         tc.tile_pool(name="held", bufs=1) as held,
         tc.tile_pool(name="scratch", bufs=2) as scratch,
-        tc.tile_pool(name="staging", bufs=4) as staging,
+        tc.tile_pool(name="staging", bufs=BLOCKS * PIECES) as staging,
         tc.psum_pool(name="psum", bufs=1) as psum,
     ):
         offsets = held.tile([P, TOKENS // 16], U16, name="offsets")
@@ -31,38 +31,55 @@ def tile_word2vec_kernel(tc, table, w, offs, out):
         w_sb = held.tile([P, BLOCKS * P], BF16, name="w_sb")
         nc.sync.dma_start(w_sb[:], w)
 
+        neg_piece_max = held.tile([P, BLOCKS, PIECES], F32, name="neg_piece_max")
+        piece_sum = held.tile([P, BLOCKS, PIECES], F32, name="piece_sum")
+
+        z = {}
         for b in range(BLOCKS):
-            z = [psum.tile([P, PIECE], F32, name=f"z_{b}_{p}") for p in range(PIECES)]
-            piece_max = held.tile([P, PIECES], F32, name=f"piece_max_{b}")
             for p in range(PIECES):
-                piece_offsets = offsets[:, p * PIECE_OFFSET_COLS : (p + 1) * PIECE_OFFSET_COLS]
+                z[b, p] = psum.tile([P, PIECE], F32, name=f"z_{b}_{p}")
                 nc.tensor.matmul(
-                    z[p][:],
+                    z[b, p][:],
                     w_sb[:, b * P : (b + 1) * P],
-                    table_sb[:].indirect(piece_offsets),
+                    table_sb[:].indirect(
+                        offsets[:, p * PIECE_OFFSET_COLS : (p + 1) * PIECE_OFFSET_COLS]
+                    ),
                     start=True,
                     stop=True,
                 )
-                nc.vector.reduce_max(piece_max[:, p : p + 1], z[p][:], axis=FREE_AXIS)
-
-            neg_max = held.tile([P, 1], F32, name=f"neg_max_{b}")
-            nc.vector.tensor_reduce(neg_max[:], piece_max[:], axis=FREE_AXIS, op=ALU.max, negate=True)
-
-            piece_sum = held.tile([P, PIECES], F32, name=f"piece_sum_{b}")
-            for p in range(PIECES):
+                nc.vector.tensor_reduce(
+                    neg_piece_max[:, b, p : p + 1], z[b, p][:], axis=FREE_AXIS, op=ALU.max, negate=True
+                )
                 exp_unused = scratch.tile([P, PIECE], F32, name="exp_unused")
                 nc.scalar.activation(
-                    exp_unused[:], z[p][:], ACT.Exp, bias=neg_max[:], scale=1.0,
-                    accum_out=piece_sum[:, p : p + 1],
+                    exp_unused[:], z[b, p][:], ACT.Exp, bias=neg_piece_max[:, b, p : p + 1], scale=1.0,
+                    accum_out=piece_sum[:, b, p : p + 1],
                 )
-            exp_sum = held.tile([P, 1], F32, name=f"exp_sum_{b}")
-            nc.vector.reduce_sum(exp_sum[:], piece_sum[:], axis=FREE_AXIS)
-            log_sum = held.tile([P, 1], F32, name=f"log_sum_{b}")
-            nc.scalar.activation(log_sum[:], exp_sum[:], ACT.Ln)
 
+        neg_max = held.tile([P, BLOCKS], F32, name="neg_max")
+        nc.vector.tensor_reduce(neg_max[:], neg_piece_max[:], axis=FREE_AXIS, op=ALU.min)
+        rescale = held.tile([P, BLOCKS, PIECES], F32, name="rescale")
+        for b in range(BLOCKS):
+            nc.scalar.activation(
+                rescale[:, b, :], neg_piece_max[:, b, :], ACT.Exp, bias=neg_max[:, b : b + 1], scale=-1.0
+            )
+        rescaled_sum = held.tile([P, BLOCKS, PIECES], F32, name="rescaled_sum")
+        nc.vector.tensor_tensor(rescaled_sum[:], piece_sum[:], rescale[:], ALU.mult)
+        exp_sum = held.tile([P, BLOCKS], F32, name="exp_sum")
+        nc.vector.reduce_sum(exp_sum[:], rescaled_sum[:], axis=FREE_AXIS)
+
+        log_sum = held.tile([P, BLOCKS], F32, name="log_sum")
+        nc.scalar.activation(log_sum[:], exp_sum[:], ACT.Ln)
+        neg_lse = held.tile([P, BLOCKS], F32, name="neg_lse")
+        nc.vector.tensor_tensor(neg_lse[:], neg_max[:], log_sum[:], ALU.subtract)
+
+        for b in range(BLOCKS):
             for p in range(PIECES):
                 result = staging.tile([P, PIECE], F32, name="result")
-                nc.vector.tensor_scalar(
-                    result[:], z[p][:], neg_max[:], log_sum[:], op0=ALU.add, op1=ALU.subtract
-                )
-                nc.sync.dma_start(out[b * P : (b + 1) * P, p * PIECE : (p + 1) * PIECE], result[:])
+                out_piece = out[b * P : (b + 1) * P, p * PIECE : (p + 1) * PIECE]
+                if p % 2 == 0:
+                    nc.vector.tensor_scalar(result[:], z[b, p][:], neg_lse[:, b : b + 1], None, op0=ALU.add)
+                    nc.sync.dma_start(out_piece, result[:])
+                else:
+                    nc.scalar.activation(result[:], z[b, p][:], ACT.Identity, bias=neg_lse[:, b : b + 1], scale=1.0)
+                    nc.scalar.dma_start(out_piece, result[:])

@@ -15,6 +15,8 @@ PIECE_OFFSET_COLS = PIECE // 16
 
 FLOPS = 2 * P * BLOCKS * P * TOKENS
 
+WARMUP_MATMULS = 6
+
 
 def tile_word2vec_kernel(tc, table, w, offs, out):
     nc = tc.nc
@@ -22,7 +24,7 @@ def tile_word2vec_kernel(tc, table, w, offs, out):
         tc.tile_pool(name="held", bufs=1) as held,
         tc.tile_pool(name="scratch", bufs=2) as scratch,
         tc.tile_pool(name="staging", bufs=BLOCKS * PIECES) as staging,
-        tc.psum_pool(name="psum", bufs=1) as psum,
+        tc.psum_pool(name="psum", bufs=BLOCKS * PIECES) as psum,
     ):
         offsets = held.tile([P, TOKENS // 16], U16, name="offsets")
         nc.sync.dma_start(offsets[:], offs)
@@ -31,13 +33,25 @@ def tile_word2vec_kernel(tc, table, w, offs, out):
         w_sb = held.tile([P, BLOCKS * P], BF16, name="w_sb")
         nc.sync.dma_start(w_sb[:], w)
 
+        zeros = held.tile([P, PIECE], BF16, name="zeros")
+        nc.vector.memset(zeros[:], 0.0)
+        warmup_ps = psum.tile([P, PIECE], F32, name="warmup_ps", tag="bank")
+        for i in range(WARMUP_MATMULS):
+            nc.tensor.matmul(warmup_ps[:], zeros[:, :P], zeros[:], start=True, stop=True)
+
         neg_piece_max = held.tile([P, BLOCKS, PIECES], F32, name="neg_piece_max")
         piece_sum = held.tile([P, BLOCKS, PIECES], F32, name="piece_sum")
+        rescale = held.tile([P, BLOCKS, PIECES], F32, name="rescale")
+        rescaled_sum = held.tile([P, BLOCKS, PIECES], F32, name="rescaled_sum")
+        neg_max = held.tile([P, BLOCKS], F32, name="neg_max")
+        exp_sum = held.tile([P, BLOCKS], F32, name="exp_sum")
+        log_sum = held.tile([P, BLOCKS], F32, name="log_sum")
+        neg_lse = held.tile([P, BLOCKS], F32, name="neg_lse")
 
         z = {}
         for b in range(BLOCKS):
             for p in range(PIECES):
-                z[b, p] = psum.tile([P, PIECE], F32, name=f"z_{b}_{p}")
+                z[b, p] = psum.tile([P, PIECE], F32, name=f"z_{b}_{p}", tag="bank")
                 nc.tensor.matmul(
                     z[b, p][:],
                     w_sb[:, b * P : (b + 1) * P],
@@ -56,21 +70,16 @@ def tile_word2vec_kernel(tc, table, w, offs, out):
                     accum_out=piece_sum[:, b, p : p + 1],
                 )
 
-        neg_max = held.tile([P, BLOCKS], F32, name="neg_max")
-        nc.vector.tensor_reduce(neg_max[:], neg_piece_max[:], axis=FREE_AXIS, op=ALU.min)
-        rescale = held.tile([P, BLOCKS, PIECES], F32, name="rescale")
-        for b in range(BLOCKS):
+            nc.vector.tensor_reduce(
+                neg_max[:, b : b + 1], neg_piece_max[:, b, :], axis=FREE_AXIS, op=ALU.min
+            )
             nc.scalar.activation(
                 rescale[:, b, :], neg_piece_max[:, b, :], ACT.Exp, bias=neg_max[:, b : b + 1], scale=-1.0
             )
-        rescaled_sum = held.tile([P, BLOCKS, PIECES], F32, name="rescaled_sum")
-        nc.vector.tensor_tensor(rescaled_sum[:], piece_sum[:], rescale[:], ALU.mult)
-        exp_sum = held.tile([P, BLOCKS], F32, name="exp_sum")
-        nc.vector.reduce_sum(exp_sum[:], rescaled_sum[:], axis=FREE_AXIS)
+            nc.vector.tensor_tensor(rescaled_sum[:, b, :], piece_sum[:, b, :], rescale[:, b, :], ALU.mult)
+            nc.vector.reduce_sum(exp_sum[:, b : b + 1], rescaled_sum[:, b, :], axis=FREE_AXIS)
 
-        log_sum = held.tile([P, BLOCKS], F32, name="log_sum")
         nc.scalar.activation(log_sum[:], exp_sum[:], ACT.Ln)
-        neg_lse = held.tile([P, BLOCKS], F32, name="neg_lse")
         nc.vector.tensor_tensor(neg_lse[:], neg_max[:], log_sum[:], ALU.subtract)
 
         for b in range(BLOCKS):

@@ -15,15 +15,13 @@ PIECE_OFFSET_COLS = PIECE // 16
 
 FLOPS = 2 * P * BLOCKS * P * TOKENS
 
-WARMUP_MATMULS = 6
-
 
 def tile_word2vec_kernel(tc, table, w, offs, out):
     nc = tc.nc
     with (
         tc.tile_pool(name="held", bufs=1) as held,
         tc.tile_pool(name="scratch", bufs=2) as scratch,
-        tc.tile_pool(name="staging", bufs=BLOCKS * PIECES) as staging,
+        tc.tile_pool(name="staging", bufs=BLOCKS * PIECES // 2) as staging,
         tc.psum_pool(name="psum", bufs=BLOCKS * PIECES) as psum,
     ):
         offsets = held.tile([P, TOKENS // 16], U16, name="offsets")
@@ -32,12 +30,6 @@ def tile_word2vec_kernel(tc, table, w, offs, out):
         nc.scalar.dma_start(table_sb[:], table)
         w_sb = held.tile([P, BLOCKS * P], BF16, name="w_sb")
         nc.sync.dma_start(w_sb[:], w)
-
-        zeros = held.tile([P, PIECE], BF16, name="zeros")
-        nc.vector.memset(zeros[:], 0.0)
-        warmup_ps = psum.tile([P, PIECE], F32, name="warmup_ps", tag="bank")
-        for i in range(WARMUP_MATMULS):
-            nc.tensor.matmul(warmup_ps[:], zeros[:, :P], zeros[:], start=True, stop=True)
 
         neg_piece_max = held.tile([P, BLOCKS, PIECES], F32, name="neg_piece_max")
         piece_sum = held.tile([P, BLOCKS, PIECES], F32, name="piece_sum")
@@ -83,12 +75,14 @@ def tile_word2vec_kernel(tc, table, w, offs, out):
         nc.vector.tensor_tensor(neg_lse[:], neg_max[:], log_sum[:], ALU.subtract)
 
         for b in range(BLOCKS):
-            for p in range(PIECES):
-                result = staging.tile([P, PIECE], F32, name="result")
-                out_piece = out[b * P : (b + 1) * P, p * PIECE : (p + 1) * PIECE]
-                if p % 2 == 0:
-                    nc.vector.tensor_scalar(result[:], z[b, p][:], neg_lse[:, b : b + 1], None, op0=ALU.add)
-                    nc.sync.dma_start(out_piece, result[:])
-                else:
-                    nc.scalar.activation(result[:], z[b, p][:], ACT.Identity, bias=neg_lse[:, b : b + 1], scale=1.0)
-                    nc.scalar.dma_start(out_piece, result[:])
+            for pair in range(PIECES // 2):
+                result = staging.tile([P, 2 * PIECE], F32, name="result")
+                nc.vector.tensor_scalar(
+                    result[:, :PIECE], z[b, 2 * pair][:], neg_lse[:, b : b + 1], None, op0=ALU.add
+                )
+                nc.scalar.activation(
+                    result[:, PIECE:], z[b, 2 * pair + 1][:], ACT.Identity, bias=neg_lse[:, b : b + 1], scale=1.0
+                )
+                nc.sync.dma_start(
+                    out[b * P : (b + 1) * P, pair * 2 * PIECE : (pair + 1) * 2 * PIECE], result[:]
+                )

@@ -33,6 +33,7 @@ def tile_word2vec_kernel(tc, table, w, offs, out):
 
         neg_piece_max = held.tile([P, BLOCKS, PIECES], F32, name="neg_piece_max")
         piece_sum = held.tile([P, BLOCKS, PIECES], F32, name="piece_sum")
+        piece_max_less_max = held.tile([P, BLOCKS, PIECES], F32, name="piece_max_less_max")
         rescale = held.tile([P, BLOCKS, PIECES], F32, name="rescale")
         rescaled_sum = held.tile([P, BLOCKS, PIECES], F32, name="rescaled_sum")
         neg_max = held.tile([P, BLOCKS], F32, name="neg_max")
@@ -62,14 +63,16 @@ def tile_word2vec_kernel(tc, table, w, offs, out):
                     accum_out=piece_sum[:, b, p : p + 1],
                 )
 
-            nc.vector.tensor_reduce(
-                neg_max[:, b : b + 1], neg_piece_max[:, b, :], axis=FREE_AXIS, op=ALU.min
-            )
-            nc.scalar.activation(
-                rescale[:, b, :], neg_piece_max[:, b, :], ACT.Exp, bias=neg_max[:, b : b + 1], scale=-1.0
-            )
-            nc.vector.tensor_tensor(rescaled_sum[:, b, :], piece_sum[:, b, :], rescale[:, b, :], ALU.mult)
-            nc.vector.reduce_sum(exp_sum[:, b : b + 1], rescaled_sum[:, b, :], axis=FREE_AXIS)
+        nc.vector.tensor_reduce(neg_max[:], neg_piece_max[:], axis=FREE_AXIS, op=ALU.min)
+        nc.vector.tensor_tensor(
+            piece_max_less_max[:],
+            neg_max[:].unsqueeze(2).to_broadcast([P, BLOCKS, PIECES]),
+            neg_piece_max[:],
+            ALU.subtract,
+        )
+        nc.scalar.activation(rescale[:], piece_max_less_max[:], ACT.Exp)
+        nc.vector.tensor_tensor(rescaled_sum[:], piece_sum[:], rescale[:], ALU.mult)
+        nc.vector.reduce_sum(exp_sum[:], rescaled_sum[:], axis=FREE_AXIS)
 
         nc.scalar.activation(log_sum[:], exp_sum[:], ACT.Ln)
         nc.vector.tensor_tensor(neg_lse[:], neg_max[:], log_sum[:], ALU.subtract)

@@ -1,6 +1,8 @@
+import math
+
 import concourse.mybir as mybir
 
-BF16, F32, U16 = mybir.dt.bfloat16, mybir.dt.float32, mybir.dt.uint16
+BF16, F32, I32, U16 = mybir.dt.bfloat16, mybir.dt.float32, mybir.dt.int32, mybir.dt.uint16
 ALU = mybir.AluOpType
 ACT = mybir.ActivationFunctionType
 FREE_AXIS = mybir.AxisListType.X
@@ -12,6 +14,13 @@ BLOCKS = 2
 PIECE = 512
 PIECES = TOKENS // PIECE
 PIECE_OFFSET_COLS = PIECE // 16
+
+MANTISSA_BITS = 23
+MANTISSA_MASK = 2 ** MANTISSA_BITS - 1
+EXPONENT_BIAS = 127
+ONE_AS_BITS = EXPONENT_BIAS * 2 ** MANTISSA_BITS
+MID = 1.5
+TERMS = 12
 
 FLOPS = 2 * P * BLOCKS * P * TOKENS
 
@@ -31,18 +40,25 @@ def tile_word2vec_kernel(tc, table, w, offs, out):
         w_sb = held.tile([P, BLOCKS * P], BF16, name="w_sb")
         nc.sync.dma_start(w_sb[:], w)
 
+        horner_addends = held.tile([P, BLOCKS, TERMS], F32, name="horner_addends")
+        for k in range(1, TERMS):
+            nc.vector.memset(horner_addends[:, :, TERMS - 1 - k : TERMS - k], (-1.0) ** k / k)
+
         neg_piece_max = held.tile([P, BLOCKS, PIECES], F32, name="neg_piece_max")
         piece_sum = held.tile([P, BLOCKS, PIECES], F32, name="piece_sum")
-        piece_max_less_max = held.tile([P, BLOCKS, PIECES], F32, name="piece_max_less_max")
         rescale = held.tile([P, BLOCKS, PIECES], F32, name="rescale")
         rescaled_sum = held.tile([P, BLOCKS, PIECES], F32, name="rescaled_sum")
         neg_max = held.tile([P, BLOCKS], F32, name="neg_max")
+        neg_max_shifted = held.tile([P, BLOCKS], F32, name="neg_max_shifted")
         exp_sum = held.tile([P, BLOCKS], F32, name="exp_sum")
-        log_sum = held.tile([P, BLOCKS], F32, name="log_sum")
-        neg_lse = held.tile([P, BLOCKS], F32, name="neg_lse")
+        mantissa = held.tile([P, BLOCKS], I32, name="mantissa")
+        exponent = held.tile([P, BLOCKS], I32, name="exponent")
+        x = held.tile([P, BLOCKS], F32, name="x")
+        horner_states = held.tile([P, BLOCKS, TERMS], F32, name="horner_states")
 
         z = {}
-        for b in range(BLOCKS):
+
+        def scores_and_sums(b):
             for p in range(PIECES):
                 z[b, p] = psum.tile([P, PIECE], F32, name=f"z_{b}_{p}", tag="bank")
                 nc.tensor.matmul(
@@ -63,29 +79,60 @@ def tile_word2vec_kernel(tc, table, w, offs, out):
                     accum_out=piece_sum[:, b, p : p + 1],
                 )
 
-        nc.vector.tensor_reduce(neg_max[:], neg_piece_max[:], axis=FREE_AXIS, op=ALU.min)
-        nc.vector.tensor_tensor(
-            piece_max_less_max[:],
-            neg_max[:].unsqueeze(2).to_broadcast([P, BLOCKS, PIECES]),
-            neg_piece_max[:],
-            ALU.subtract,
-        )
-        nc.scalar.activation(rescale[:], piece_max_less_max[:], ACT.Exp)
-        nc.vector.tensor_tensor(rescaled_sum[:], piece_sum[:], rescale[:], ALU.mult)
-        nc.vector.reduce_sum(exp_sum[:], rescaled_sum[:], axis=FREE_AXIS)
+        def neg_log_sum_exp(b):
+            one = slice(b, b + 1)
+            nc.vector.tensor_reduce(neg_max[:, one], neg_piece_max[:, b, :], axis=FREE_AXIS, op=ALU.min)
+            nc.scalar.activation(
+                rescale[:, b, :], neg_piece_max[:, b, :], ACT.Exp, bias=neg_max[:, one], scale=-1.0
+            )
+            nc.vector.scalar_tensor_tensor(
+                rescaled_sum[:, b, :], piece_sum[:, b, :], 1.0, rescale[:, b, :],
+                op0=ALU.mult, op1=ALU.mult, accum_out=exp_sum[:, one],
+            )
+            bits = exp_sum[:, one].bitcast(I32)
+            nc.vector.tensor_scalar(
+                mantissa[:, one], bits, MANTISSA_MASK, ONE_AS_BITS, op0=ALU.bitwise_and, op1=ALU.bitwise_or
+            )
+            nc.vector.tensor_scalar(
+                exponent[:, one], bits, MANTISSA_BITS, None, op0=ALU.logical_shift_right
+            )
+            nc.vector.tensor_scalar(
+                x[:, one], mantissa[:, one].bitcast(F32), 1.0 / MID, -1.0, op0=ALU.mult, op1=ALU.add
+            )
+            nc.vector.tensor_scalar(
+                neg_max_shifted[:, one], neg_max[:, one],
+                EXPONENT_BIAS * math.log(2.0) - math.log(MID), None, op0=ALU.add,
+            )
+            nc.vector.tensor_scalar(
+                horner_addends[:, b, TERMS - 1 : TERMS], exponent[:, one], -math.log(2.0),
+                neg_max_shifted[:, one], op0=ALU.mult, op1=ALU.add,
+            )
+            nc.vector.tensor_tensor_scan(
+                horner_states[:, b, :], x[:, one].to_broadcast([P, TERMS]), horner_addends[:, b, :],
+                (-1.0) ** TERMS / TERMS, op0=ALU.mult, op1=ALU.add,
+            )
+            return horner_states[:, b, TERMS - 1 : TERMS]
 
-        nc.scalar.activation(log_sum[:], exp_sum[:], ACT.Ln)
-        nc.vector.tensor_tensor(neg_lse[:], neg_max[:], log_sum[:], ALU.subtract)
-
-        for b in range(BLOCKS):
+        def subtract_and_store(b, neg_lse, engines):
             for pair in range(PIECES // 2):
                 result = staging.tile([P, 2 * PIECE], F32, name="result")
-                nc.vector.tensor_scalar(
-                    result[:, :PIECE], z[b, 2 * pair][:], neg_lse[:, b : b + 1], None, op0=ALU.add
-                )
-                nc.scalar.activation(
-                    result[:, PIECE:], z[b, 2 * pair + 1][:], ACT.Identity, bias=neg_lse[:, b : b + 1], scale=1.0
-                )
+                for half in range(2):
+                    columns = slice(half * PIECE, (half + 1) * PIECE)
+                    if engines[half] == "vector":
+                        nc.vector.tensor_scalar(
+                            result[:, columns], z[b, 2 * pair + half][:], neg_lse, None, op0=ALU.add
+                        )
+                    else:
+                        nc.scalar.activation(
+                            result[:, columns], z[b, 2 * pair + half][:], ACT.Identity, bias=neg_lse, scale=1.0
+                        )
                 nc.sync.dma_start(
                     out[b * P : (b + 1) * P, pair * 2 * PIECE : (pair + 1) * 2 * PIECE], result[:]
                 )
+
+        scores_and_sums(0)
+        neg_lse_0 = neg_log_sum_exp(0)
+        scores_and_sums(1)
+        neg_lse_1 = neg_log_sum_exp(1)
+        subtract_and_store(0, neg_lse_0, ("vector", "scalar"))
+        subtract_and_store(1, neg_lse_1, ("vector", "scalar"))

@@ -21,6 +21,8 @@ EXPONENT_BIAS = 127
 ONE_AS_BITS = EXPONENT_BIAS * 2 ** MANTISSA_BITS
 MID = 1.5
 TERMS = 12
+SUM_SCALE = 2.0 * MID
+LOW_SEVEN_BITS = 127
 
 FLOPS = 2 * P * BLOCKS * P * TOKENS
 
@@ -49,8 +51,7 @@ def tile_word2vec_kernel(tc, table, w, offs, out):
         rescale = held.tile([P, BLOCKS, PIECES], F32, name="rescale")
         rescaled_sum = held.tile([P, BLOCKS, PIECES], F32, name="rescaled_sum")
         neg_max = held.tile([P, BLOCKS], F32, name="neg_max")
-        neg_max_shifted = held.tile([P, BLOCKS], F32, name="neg_max_shifted")
-        exp_sum = held.tile([P, BLOCKS], F32, name="exp_sum")
+        scaled_exp_sum = held.tile([P, BLOCKS], F32, name="scaled_exp_sum")
         mantissa = held.tile([P, BLOCKS], I32, name="mantissa")
         exponent = held.tile([P, BLOCKS], I32, name="exponent")
         x = held.tile([P, BLOCKS], F32, name="x")
@@ -86,26 +87,23 @@ def tile_word2vec_kernel(tc, table, w, offs, out):
                 rescale[:, b, :], neg_piece_max[:, b, :], ACT.Exp, bias=neg_max[:, one], scale=-1.0
             )
             nc.vector.scalar_tensor_tensor(
-                rescaled_sum[:, b, :], piece_sum[:, b, :], 1.0, rescale[:, b, :],
-                op0=ALU.mult, op1=ALU.mult, accum_out=exp_sum[:, one],
+                rescaled_sum[:, b, :], piece_sum[:, b, :], SUM_SCALE, rescale[:, b, :],
+                op0=ALU.mult, op1=ALU.mult, accum_out=scaled_exp_sum[:, one],
             )
-            bits = exp_sum[:, one].bitcast(I32)
+            bits = scaled_exp_sum[:, one].bitcast(I32)
             nc.vector.tensor_scalar(
                 mantissa[:, one], bits, MANTISSA_MASK, ONE_AS_BITS, op0=ALU.bitwise_and, op1=ALU.bitwise_or
             )
             nc.vector.tensor_scalar(
-                exponent[:, one], bits, MANTISSA_BITS, None, op0=ALU.logical_shift_right
+                exponent[:, one], bits, MANTISSA_BITS, LOW_SEVEN_BITS,
+                op0=ALU.logical_shift_right, op1=ALU.bitwise_and,
             )
             nc.vector.tensor_scalar(
                 x[:, one], mantissa[:, one].bitcast(F32), 1.0 / MID, -1.0, op0=ALU.mult, op1=ALU.add
             )
             nc.vector.tensor_scalar(
-                neg_max_shifted[:, one], neg_max[:, one],
-                EXPONENT_BIAS * math.log(2.0) - math.log(MID), None, op0=ALU.add,
-            )
-            nc.vector.tensor_scalar(
                 horner_addends[:, b, TERMS - 1 : TERMS], exponent[:, one], -math.log(2.0),
-                neg_max_shifted[:, one], op0=ALU.mult, op1=ALU.add,
+                neg_max[:, one], op0=ALU.mult, op1=ALU.add,
             )
             nc.vector.tensor_tensor_scan(
                 horner_states[:, b, :], x[:, one].to_broadcast([P, TERMS]), horner_addends[:, b, :],
@@ -113,19 +111,15 @@ def tile_word2vec_kernel(tc, table, w, offs, out):
             )
             return horner_states[:, b, TERMS - 1 : TERMS]
 
-        def subtract_and_store(b, neg_lse, engines):
+        def subtract_and_store(b, neg_lse):
             for pair in range(PIECES // 2):
                 result = staging.tile([P, 2 * PIECE], F32, name="result")
-                for half in range(2):
-                    columns = slice(half * PIECE, (half + 1) * PIECE)
-                    if engines[half] == "vector":
-                        nc.vector.tensor_scalar(
-                            result[:, columns], z[b, 2 * pair + half][:], neg_lse, None, op0=ALU.add
-                        )
-                    else:
-                        nc.scalar.activation(
-                            result[:, columns], z[b, 2 * pair + half][:], ACT.Identity, bias=neg_lse, scale=1.0
-                        )
+                nc.vector.tensor_scalar(
+                    result[:, :PIECE], z[b, 2 * pair][:], neg_lse, None, op0=ALU.add
+                )
+                nc.scalar.activation(
+                    result[:, PIECE:], z[b, 2 * pair + 1][:], ACT.Identity, bias=neg_lse, scale=1.0
+                )
                 nc.sync.dma_start(
                     out[b * P : (b + 1) * P, pair * 2 * PIECE : (pair + 1) * 2 * PIECE], result[:]
                 )
@@ -134,5 +128,5 @@ def tile_word2vec_kernel(tc, table, w, offs, out):
         neg_lse_0 = neg_log_sum_exp(0)
         scores_and_sums(1)
         neg_lse_1 = neg_log_sum_exp(1)
-        subtract_and_store(0, neg_lse_0, ("vector", "scalar"))
-        subtract_and_store(1, neg_lse_1, ("vector", "scalar"))
+        subtract_and_store(0, neg_lse_0)
+        subtract_and_store(1, neg_lse_1)

@@ -38,7 +38,7 @@ def tile_word2vec_kernel(tc, table, w, offs, out):
         offsets = held.tile([P, TOKENS // 16], U16, name="offsets")
         nc.sync.dma_start(offsets[:], offs)
         table_sb = held.tile([P, WORDS], BF16, name="table_sb")
-        nc.scalar.dma_start(table_sb[:], table)
+        nc.sync.dma_start(table_sb[:], table)
         w_sb = held.tile([P, BLOCKS * P], BF16, name="w_sb")
         nc.sync.dma_start(w_sb[:], w)
 

@@ -50,6 +50,7 @@ def tile_word2vec_kernel(tc, table, w, offs, out):
         piece_sum = held.tile([P, BLOCKS, PIECES], F32, name="piece_sum")
         rescale = held.tile([P, BLOCKS, PIECES], F32, name="rescale")
         rescaled_sum = held.tile([P, BLOCKS, PIECES], F32, name="rescaled_sum")
+        neg_max_but_last = held.tile([P, BLOCKS], F32, name="neg_max_but_last")
         neg_max = held.tile([P, BLOCKS], F32, name="neg_max")
         scaled_exp_sum = held.tile([P, BLOCKS], F32, name="scaled_exp_sum")
         mantissa = held.tile([P, BLOCKS], I32, name="mantissa")
@@ -80,9 +81,15 @@ def tile_word2vec_kernel(tc, table, w, offs, out):
                     accum_out=piece_sum[:, b, p : p + 1],
                 )
 
-        def neg_log_sum_exp(b):
+        def neg_log_sum_exp(b, max_engine):
             one = slice(b, b + 1)
-            nc.vector.tensor_reduce(neg_max[:, one], neg_piece_max[:, b, :], axis=FREE_AXIS, op=ALU.min)
+            max_engine.tensor_scalar(
+                neg_max_but_last[:, one], neg_piece_max[:, b, 0:1], neg_piece_max[:, b, 1:2],
+                neg_piece_max[:, b, 2:3], op0=ALU.min, op1=ALU.min,
+            )
+            max_engine.tensor_scalar(
+                neg_max[:, one], neg_max_but_last[:, one], neg_piece_max[:, b, 3:4], None, op0=ALU.min
+            )
             nc.scalar.activation(
                 rescale[:, b, :], neg_piece_max[:, b, :], ACT.Exp, bias=neg_max[:, one], scale=-1.0
             )
@@ -125,8 +132,8 @@ def tile_word2vec_kernel(tc, table, w, offs, out):
                 )
 
         scores_and_sums(0)
-        neg_lse_0 = neg_log_sum_exp(0)
+        neg_lse_0 = neg_log_sum_exp(0, nc.vector)
         scores_and_sums(1)
-        neg_lse_1 = neg_log_sum_exp(1)
+        neg_lse_1 = neg_log_sum_exp(1, nc.gpsimd)
         subtract_and_store(0, neg_lse_0)
         subtract_and_store(1, neg_lse_1)

@@ -50,7 +50,7 @@ def tile_word2vec_kernel(tc, table, w, offs, out):
         piece_sum = held.tile([P, BLOCKS, PIECES], F32, name="piece_sum")
         rescale = held.tile([P, BLOCKS, PIECES], F32, name="rescale")
         rescaled_sum = held.tile([P, BLOCKS, PIECES], F32, name="rescaled_sum")
-        neg_max_but_last = held.tile([P, BLOCKS], F32, name="neg_max_but_last")
+        neg_max_but_last = held.tile([P, 1], F32, name="neg_max_but_last")
         neg_max = held.tile([P, BLOCKS], F32, name="neg_max")
         scaled_exp_sum = held.tile([P, BLOCKS], F32, name="scaled_exp_sum")
         mantissa = held.tile([P, BLOCKS], I32, name="mantissa")
@@ -81,14 +81,14 @@ def tile_word2vec_kernel(tc, table, w, offs, out):
                     accum_out=piece_sum[:, b, p : p + 1],
                 )
 
-        def neg_log_sum_exp(b, max_engine):
+        def neg_log_sum_exp(b):
             one = slice(b, b + 1)
-            max_engine.tensor_scalar(
-                neg_max_but_last[:, one], neg_piece_max[:, b, 0:1], neg_piece_max[:, b, 1:2],
+            nc.gpsimd.tensor_scalar(
+                neg_max_but_last[:], neg_piece_max[:, b, 0:1], neg_piece_max[:, b, 1:2],
                 neg_piece_max[:, b, 2:3], op0=ALU.min, op1=ALU.min,
             )
-            max_engine.tensor_scalar(
-                neg_max[:, one], neg_max_but_last[:, one], neg_piece_max[:, b, 3:4], None, op0=ALU.min
+            nc.gpsimd.tensor_scalar(
+                neg_max[:, one], neg_max_but_last[:], neg_piece_max[:, b, 3:4], None, op0=ALU.min
             )
             nc.scalar.activation(
                 rescale[:, b, :], neg_piece_max[:, b, :], ACT.Exp, bias=neg_max[:, one], scale=-1.0
@@ -132,8 +132,8 @@ def tile_word2vec_kernel(tc, table, w, offs, out):
                 )
 
         scores_and_sums(0)
-        neg_lse_0 = neg_log_sum_exp(0, nc.vector)
+        neg_lse_0 = neg_log_sum_exp(0)
         scores_and_sums(1)
-        neg_lse_1 = neg_log_sum_exp(1, nc.gpsimd)
+        neg_lse_1 = neg_log_sum_exp(1)
         subtract_and_store(0, neg_lse_0)
         subtract_and_store(1, neg_lse_1)

@@ -19,10 +19,25 @@ MANTISSA_BITS = 23
 MANTISSA_MASK = 2 ** MANTISSA_BITS - 1
 EXPONENT_BIAS = 127
 ONE_AS_BITS = EXPONENT_BIAS * 2 ** MANTISSA_BITS
-MID = 1.5
-TERMS = 12
-SUM_SCALE = 2.0 * MID
-LOW_SEVEN_BITS = 127
+LN2 = math.log(2.0)
+SUM_EXPONENT_SHIFT = 96
+DEGREE = 6
+
+
+def log_correction_coefficients():
+    n = DEGREE + 1
+    nodes = [1.5 + 0.5 * math.cos(math.pi * (2 * i + 1) / (2 * n)) for i in range(n)]
+    differences = [LN2 * u - math.log(u) for u in nodes]
+    for order in range(1, n):
+        for i in range(n - 1, order - 1, -1):
+            differences[i] = (differences[i] - differences[i - 1]) / (nodes[i] - nodes[i - order])
+    coefficients = [0.0] * n
+    for i in range(n - 1, -1, -1):
+        shifted = [0.0] + coefficients[:-1]
+        coefficients = [shifted[k] - nodes[i] * coefficients[k] for k in range(n)]
+        coefficients[0] += differences[i]
+    return coefficients
+
 
 FLOPS = 2 * P * BLOCKS * P * TOKENS
 
@@ -42,9 +57,10 @@ def tile_word2vec_kernel(tc, table, w, offs, out):
         w_sb = held.tile([P, BLOCKS * P], BF16, name="w_sb")
         nc.sync.dma_start(w_sb[:], w)
 
-        horner_addends = held.tile([P, BLOCKS, TERMS], F32, name="horner_addends")
-        for k in range(1, TERMS):
-            nc.vector.memset(horner_addends[:, :, TERMS - 1 - k : TERMS - k], (-1.0) ** k / k)
+        coefficients = log_correction_coefficients()
+        horner_addends = held.tile([P, BLOCKS, DEGREE], F32, name="horner_addends")
+        for k in range(1, DEGREE):
+            nc.vector.memset(horner_addends[:, :, DEGREE - 1 - k : DEGREE - k], coefficients[k])
 
         neg_piece_max = held.tile([P, BLOCKS, PIECES], F32, name="neg_piece_max")
         piece_sum = held.tile([P, BLOCKS, PIECES], F32, name="piece_sum")
@@ -52,11 +68,10 @@ def tile_word2vec_kernel(tc, table, w, offs, out):
         rescaled_sum = held.tile([P, BLOCKS, PIECES], F32, name="rescaled_sum")
         neg_max_but_last = held.tile([P, 1], F32, name="neg_max_but_last")
         neg_max = held.tile([P, BLOCKS], F32, name="neg_max")
+        constant_minus_max = held.tile([P, BLOCKS], F32, name="constant_minus_max")
         scaled_exp_sum = held.tile([P, BLOCKS], F32, name="scaled_exp_sum")
-        mantissa = held.tile([P, BLOCKS], I32, name="mantissa")
-        exponent = held.tile([P, BLOCKS], I32, name="exponent")
-        x = held.tile([P, BLOCKS], F32, name="x")
-        horner_states = held.tile([P, BLOCKS, TERMS], F32, name="horner_states")
+        u_bits = held.tile([P, BLOCKS], I32, name="u_bits")
+        horner_states = held.tile([P, BLOCKS, DEGREE], F32, name="horner_states")
 
         z = {}
 
@@ -90,33 +105,30 @@ def tile_word2vec_kernel(tc, table, w, offs, out):
             nc.gpsimd.tensor_scalar(
                 neg_max[:, one], neg_max_but_last[:], neg_piece_max[:, b, 3:4], None, op0=ALU.min
             )
+            nc.gpsimd.tensor_scalar(
+                constant_minus_max[:, one], neg_max[:, one],
+                (EXPONENT_BIAS - 1 - SUM_EXPONENT_SHIFT) * LN2 + coefficients[0], None, op0=ALU.add,
+            )
             nc.scalar.activation(
                 rescale[:, b, :], neg_piece_max[:, b, :], ACT.Exp, bias=neg_max[:, one], scale=-1.0
             )
             nc.vector.scalar_tensor_tensor(
-                rescaled_sum[:, b, :], piece_sum[:, b, :], SUM_SCALE, rescale[:, b, :],
+                rescaled_sum[:, b, :], piece_sum[:, b, :], 2.0 ** -SUM_EXPONENT_SHIFT, rescale[:, b, :],
                 op0=ALU.mult, op1=ALU.mult, accum_out=scaled_exp_sum[:, one],
             )
             bits = scaled_exp_sum[:, one].bitcast(I32)
             nc.vector.tensor_scalar(
-                mantissa[:, one], bits, MANTISSA_MASK, ONE_AS_BITS, op0=ALU.bitwise_and, op1=ALU.bitwise_or
+                u_bits[:, one], bits, MANTISSA_MASK, ONE_AS_BITS, op0=ALU.bitwise_and, op1=ALU.bitwise_or
             )
             nc.vector.tensor_scalar(
-                exponent[:, one], bits, MANTISSA_BITS, LOW_SEVEN_BITS,
-                op0=ALU.logical_shift_right, op1=ALU.bitwise_and,
-            )
-            nc.vector.tensor_scalar(
-                x[:, one], mantissa[:, one].bitcast(F32), 1.0 / MID, -1.0, op0=ALU.mult, op1=ALU.add
-            )
-            nc.vector.tensor_scalar(
-                horner_addends[:, b, TERMS - 1 : TERMS], exponent[:, one], -math.log(2.0),
-                neg_max[:, one], op0=ALU.mult, op1=ALU.add,
+                horner_addends[:, b, DEGREE - 1 : DEGREE], bits, -LN2 / 2 ** MANTISSA_BITS,
+                constant_minus_max[:, one], op0=ALU.mult, op1=ALU.add,
             )
             nc.vector.tensor_tensor_scan(
-                horner_states[:, b, :], x[:, one].to_broadcast([P, TERMS]), horner_addends[:, b, :],
-                (-1.0) ** TERMS / TERMS, op0=ALU.mult, op1=ALU.add,
+                horner_states[:, b, :], u_bits[:, one].bitcast(F32).to_broadcast([P, DEGREE]),
+                horner_addends[:, b, :], coefficients[DEGREE], op0=ALU.mult, op1=ALU.add,
             )
-            return horner_states[:, b, TERMS - 1 : TERMS]
+            return horner_states[:, b, DEGREE - 1 : DEGREE]
 
         def subtract_and_store(b, neg_lse):
             for pair in range(PIECES // 2):

@@ -14,6 +14,7 @@ BLOCKS = 2
 PIECE = 512
 PIECES = TOKENS // PIECE
 PIECE_OFFSET_COLS = PIECE // 16
+SUM_BEFORE_PIECE = PIECES - 1
 
 MANTISSA_BITS = 23
 MANTISSA_MASK = 2 ** MANTISSA_BITS - 1
@@ -62,10 +63,11 @@ def tile_word2vec_kernel(tc, table, w, offs, out):
         for k in range(1, DEGREE):
             nc.vector.memset(horner_addends[:, :, DEGREE - 1 - k : DEGREE - k], coefficients[k])
 
-        neg_piece_max = held.tile([P, BLOCKS, PIECES], F32, name="neg_piece_max")
+        neg_piece_max = [
+            held.tile([P, SUM_BEFORE_PIECE + PIECES], F32, name=f"neg_piece_max_{b}") for b in range(BLOCKS + 1)
+        ]
         piece_sum = held.tile([P, BLOCKS, PIECES], F32, name="piece_sum")
         rescale = held.tile([P, BLOCKS, PIECES], F32, name="rescale")
-        rescaled_sum = held.tile([P, BLOCKS, PIECES], F32, name="rescaled_sum")
         neg_max_but_last = held.tile([P, 1], F32, name="neg_max_but_last")
         neg_max = held.tile([P, BLOCKS], F32, name="neg_max")
         constant_minus_max = held.tile([P, BLOCKS], F32, name="constant_minus_max")
@@ -88,32 +90,32 @@ def tile_word2vec_kernel(tc, table, w, offs, out):
                     stop=True,
                 )
                 nc.vector.tensor_reduce(
-                    neg_piece_max[:, b, p : p + 1], z[b, p][:], axis=FREE_AXIS, op=ALU.max, negate=True
+                    neg_piece_max[b][:, p : p + 1], z[b, p][:], axis=FREE_AXIS, op=ALU.max, negate=True
                 )
                 exp_unused = scratch.tile([P, PIECE], F32, name="exp_unused")
                 nc.scalar.activation(
-                    exp_unused[:], z[b, p][:], ACT.Exp, bias=neg_piece_max[:, b, p : p + 1], scale=1.0,
+                    exp_unused[:], z[b, p][:], ACT.Exp, bias=neg_piece_max[b][:, p : p + 1], scale=1.0,
                     accum_out=piece_sum[:, b, p : p + 1],
                 )
 
         def neg_log_sum_exp(b):
             one = slice(b, b + 1)
             nc.gpsimd.tensor_scalar(
-                neg_max_but_last[:], neg_piece_max[:, b, 0:1], neg_piece_max[:, b, 1:2],
-                neg_piece_max[:, b, 2:3], op0=ALU.min, op1=ALU.min,
+                neg_max_but_last[:], neg_piece_max[b][:, 0:1], neg_piece_max[b][:, 1:2],
+                neg_piece_max[b][:, 2:3], op0=ALU.min, op1=ALU.min,
             )
             nc.gpsimd.tensor_scalar(
-                neg_max[:, one], neg_max_but_last[:], neg_piece_max[:, b, 3:4], None, op0=ALU.min
+                neg_max[:, one], neg_max_but_last[:], neg_piece_max[b][:, 3:4], None, op0=ALU.min
             )
             nc.gpsimd.tensor_scalar(
                 constant_minus_max[:, one], neg_max[:, one],
                 (EXPONENT_BIAS - 1 - SUM_EXPONENT_SHIFT) * LN2 + coefficients[0], None, op0=ALU.add,
             )
             nc.scalar.activation(
-                rescale[:, b, :], neg_piece_max[:, b, :], ACT.Exp, bias=neg_max[:, one], scale=-1.0
+                rescale[:, b, :], neg_piece_max[b][:, :PIECES], ACT.Exp, bias=neg_max[:, one], scale=-1.0
             )
             nc.vector.scalar_tensor_tensor(
-                rescaled_sum[:, b, :], piece_sum[:, b, :], 2.0 ** -SUM_EXPONENT_SHIFT, rescale[:, b, :],
+                neg_piece_max[b + 1][:, SUM_BEFORE_PIECE : SUM_BEFORE_PIECE + PIECES], piece_sum[:, b, :], 2.0 ** -SUM_EXPONENT_SHIFT, rescale[:, b, :],
                 op0=ALU.mult, op1=ALU.mult, accum_out=scaled_exp_sum[:, one],
             )
             bits = scaled_exp_sum[:, one].bitcast(I32)
@@ -130,22 +132,36 @@ def tile_word2vec_kernel(tc, table, w, offs, out):
             )
             return horner_states[:, b, DEGREE - 1 : DEGREE]
 
-        def subtract_and_store(b, neg_lse):
-            for pair in range(PIECES // 2):
+        def vector_subtract(result, b, p, neg_lse):
+            nc.vector.tensor_scalar(result, z[b, p][:], neg_lse, None, op0=ALU.add)
+
+        def scalar_subtract(result, b, p, neg_lse):
+            nc.scalar.activation(result, z[b, p][:], ACT.Identity, bias=neg_lse, scale=1.0)
+
+        def store(result, b, first_piece, pieces):
+            tokens = slice(first_piece * PIECE, (first_piece + pieces) * PIECE)
+            nc.sync.dma_start(out[b * P : (b + 1) * P, tokens], result)
+
+        def finish_first_block(b, neg_lse):
+            for p in range(PIECES // 2):
+                early = staging.tile([P, PIECE], F32, name="early")
+                vector_subtract(early[:], b, p, neg_lse)
+                store(early[:], b, p, 1)
+            late = staging.tile([P, 2 * PIECE], F32, name="result")
+            for i in range(PIECES // 2):
+                scalar_subtract(late[:, i * PIECE : (i + 1) * PIECE], b, PIECES // 2 + i, neg_lse)
+            store(late[:], b, PIECES // 2, PIECES // 2)
+
+        def finish_last_block(b, neg_lse):
+            for p in range(0, PIECES, 2):
                 result = staging.tile([P, 2 * PIECE], F32, name="result")
-                nc.vector.tensor_scalar(
-                    result[:, :PIECE], z[b, 2 * pair][:], neg_lse, None, op0=ALU.add
-                )
-                nc.scalar.activation(
-                    result[:, PIECE:], z[b, 2 * pair + 1][:], ACT.Identity, bias=neg_lse, scale=1.0
-                )
-                nc.sync.dma_start(
-                    out[b * P : (b + 1) * P, pair * 2 * PIECE : (pair + 1) * 2 * PIECE], result[:]
-                )
+                vector_subtract(result[:, :PIECE], b, p, neg_lse)
+                scalar_subtract(result[:, PIECE:], b, p + 1, neg_lse)
+                store(result[:], b, p, 2)
 
         scores_and_sums(0)
         neg_lse_0 = neg_log_sum_exp(0)
         scores_and_sums(1)
         neg_lse_1 = neg_log_sum_exp(1)
-        subtract_and_store(0, neg_lse_0)
-        subtract_and_store(1, neg_lse_1)
+        finish_first_block(0, neg_lse_0)
+        finish_last_block(1, neg_lse_1)

@@ -143,14 +143,16 @@ def tile_word2vec_kernel(tc, table, w, offs, out):
             nc.sync.dma_start(out[b * P : (b + 1) * P, tokens], result)
 
         def finish_first_block(b, neg_lse):
-            for p in range(PIECES // 2):
-                early = staging.tile([P, PIECE], F32, name="early")
-                vector_subtract(early[:], b, p, neg_lse)
-                store(early[:], b, p, 1)
-            late = staging.tile([P, 2 * PIECE], F32, name="result")
-            for i in range(PIECES // 2):
-                scalar_subtract(late[:, i * PIECE : (i + 1) * PIECE], b, PIECES // 2 + i, neg_lse)
-            store(late[:], b, PIECES // 2, PIECES // 2)
+            first = staging.tile([P, PIECE], F32, name="first")
+            vector_subtract(first[:], b, 0, neg_lse)
+            store(first[:], b, 0, 1)
+            middle = staging.tile([P, 2 * PIECE], F32, name="middle")
+            vector_subtract(middle[:, :PIECE], b, 1, neg_lse)
+            scalar_subtract(middle[:, PIECE:], b, 2, neg_lse)
+            store(middle[:], b, 1, 2)
+            last = staging.tile([P, PIECE], F32, name="last")
+            scalar_subtract(last[:], b, 3, neg_lse)
+            store(last[:], b, 3, 1)
 
         def finish_last_block(b, neg_lse):
             for p in range(0, PIECES, 2):

import math

import concourse.mybir as mybir

BF16, F32, I32, U16 = mybir.dt.bfloat16, mybir.dt.float32, mybir.dt.int32, mybir.dt.uint16
ALU = mybir.AluOpType
ACT = mybir.ActivationFunctionType
FREE_AXIS = mybir.AxisListType.X

P = 128
WORDS = 1024
TOKENS = 2048
BLOCKS = 2
PIECE = 512
PIECES = TOKENS // PIECE
PIECE_OFFSET_COLS = PIECE // 16
SUM_BEFORE_PIECE = PIECES - 1

MANTISSA_BITS = 23
MANTISSA_MASK = 2 ** MANTISSA_BITS - 1
EXPONENT_BIAS = 127
ONE_AS_BITS = EXPONENT_BIAS * 2 ** MANTISSA_BITS
LN2 = math.log(2.0)
SUM_EXPONENT_SHIFT = 96
DEGREE = 6


def log_correction_coefficients():
    n = DEGREE + 1
    nodes = [1.5 + 0.5 * math.cos(math.pi * (2 * i + 1) / (2 * n)) for i in range(n)]
    differences = [LN2 * u - math.log(u) for u in nodes]
    for order in range(1, n):
        for i in range(n - 1, order - 1, -1):
            differences[i] = (differences[i] - differences[i - 1]) / (nodes[i] - nodes[i - order])
    coefficients = [0.0] * n
    for i in range(n - 1, -1, -1):
        shifted = [0.0] + coefficients[:-1]
        coefficients = [shifted[k] - nodes[i] * coefficients[k] for k in range(n)]
        coefficients[0] += differences[i]
    return coefficients


FLOPS = 2 * P * BLOCKS * P * TOKENS


def tile_word2vec_kernel(tc, table, w, offs, out):
    nc = tc.nc
    with (
        tc.tile_pool(name="held", bufs=1) as held,
        tc.tile_pool(name="scratch", bufs=2) as scratch,
        tc.tile_pool(name="staging", bufs=BLOCKS * PIECES // 2) as staging,
        tc.psum_pool(name="psum", bufs=BLOCKS * PIECES) as psum,
    ):
        offsets = held.tile([P, TOKENS // 16], U16, name="offsets")
        nc.sync.dma_start(offsets[:], offs)
        table_sb = held.tile([P, WORDS], BF16, name="table_sb")
        nc.sync.dma_start(table_sb[:], table)
        w_sb = held.tile([P, BLOCKS * P], BF16, name="w_sb")
        nc.sync.dma_start(w_sb[:], w)

        coefficients = log_correction_coefficients()
        horner_addends = held.tile([P, BLOCKS, DEGREE], F32, name="horner_addends")
        for k in range(1, DEGREE):
            nc.vector.memset(horner_addends[:, :, DEGREE - 1 - k : DEGREE - k], coefficients[k])

        neg_piece_max = [
            held.tile([P, SUM_BEFORE_PIECE + PIECES], F32, name=f"neg_piece_max_{b}") for b in range(BLOCKS + 1)
        ]
        piece_sum = held.tile([P, BLOCKS, PIECES], F32, name="piece_sum")
        rescale = held.tile([P, BLOCKS, PIECES], F32, name="rescale")
        neg_max_but_last = held.tile([P, 1], F32, name="neg_max_but_last")
        neg_max = held.tile([P, BLOCKS], F32, name="neg_max")
        constant_minus_max = held.tile([P, BLOCKS], F32, name="constant_minus_max")
        scaled_exp_sum = held.tile([P, BLOCKS], F32, name="scaled_exp_sum")
        u_bits = held.tile([P, BLOCKS], I32, name="u_bits")
        horner_states = held.tile([P, BLOCKS, DEGREE], F32, name="horner_states")

        z = {}

        def scores_and_sums(b):
            for p in range(PIECES):
                z[b, p] = psum.tile([P, PIECE], F32, name=f"z_{b}_{p}", tag="bank")
                nc.tensor.matmul(
                    z[b, p][:],
                    w_sb[:, b * P : (b + 1) * P],
                    table_sb[:].indirect(
                        offsets[:, p * PIECE_OFFSET_COLS : (p + 1) * PIECE_OFFSET_COLS]
                    ),
                    start=True,
                    stop=True,
                )
                nc.vector.tensor_reduce(
                    neg_piece_max[b][:, p : p + 1], z[b, p][:], axis=FREE_AXIS, op=ALU.max, negate=True
                )
                exp_unused = scratch.tile([P, PIECE], F32, name="exp_unused")
                nc.scalar.activation(
                    exp_unused[:], z[b, p][:], ACT.Exp, bias=neg_piece_max[b][:, p : p + 1], scale=1.0,
                    accum_out=piece_sum[:, b, p : p + 1],
                )

        def neg_log_sum_exp(b):
            one = slice(b, b + 1)
            nc.gpsimd.tensor_scalar(
                neg_max_but_last[:], neg_piece_max[b][:, 0:1], neg_piece_max[b][:, 1:2],
                neg_piece_max[b][:, 2:3], op0=ALU.min, op1=ALU.min,
            )
            nc.gpsimd.tensor_scalar(
                neg_max[:, one], neg_max_but_last[:], neg_piece_max[b][:, 3:4], None, op0=ALU.min
            )
            nc.gpsimd.tensor_scalar(
                constant_minus_max[:, one], neg_max[:, one],
                (EXPONENT_BIAS - 1 - SUM_EXPONENT_SHIFT) * LN2 + coefficients[0], None, op0=ALU.add,
            )
            nc.scalar.activation(
                rescale[:, b, :], neg_piece_max[b][:, :PIECES], ACT.Exp, bias=neg_max[:, one], scale=-1.0
            )
            nc.vector.scalar_tensor_tensor(
                neg_piece_max[b + 1][:, SUM_BEFORE_PIECE : SUM_BEFORE_PIECE + PIECES], piece_sum[:, b, :], 2.0 ** -SUM_EXPONENT_SHIFT, rescale[:, b, :],
                op0=ALU.mult, op1=ALU.mult, accum_out=scaled_exp_sum[:, one],
            )
            bits = scaled_exp_sum[:, one].bitcast(I32)
            nc.vector.tensor_scalar(
                u_bits[:, one], bits, MANTISSA_MASK, ONE_AS_BITS, op0=ALU.bitwise_and, op1=ALU.bitwise_or
            )
            nc.vector.tensor_scalar(
                horner_addends[:, b, DEGREE - 1 : DEGREE], bits, -LN2 / 2 ** MANTISSA_BITS,
                constant_minus_max[:, one], op0=ALU.mult, op1=ALU.add,
            )
            nc.vector.tensor_tensor_scan(
                horner_states[:, b, :], u_bits[:, one].bitcast(F32).to_broadcast([P, DEGREE]),
                horner_addends[:, b, :], coefficients[DEGREE], op0=ALU.mult, op1=ALU.add,
            )
            return horner_states[:, b, DEGREE - 1 : DEGREE]

        def vector_subtract(result, b, p, neg_lse):
            nc.vector.tensor_scalar(result, z[b, p][:], neg_lse, None, op0=ALU.add)

        def scalar_subtract(result, b, p, neg_lse):
            nc.scalar.activation(result, z[b, p][:], ACT.Identity, bias=neg_lse, scale=1.0)

        def store(result, b, first_piece, pieces):
            tokens = slice(first_piece * PIECE, (first_piece + pieces) * PIECE)
            nc.sync.dma_start(out[b * P : (b + 1) * P, tokens], result)

        def finish_first_block(b, neg_lse):
            first = staging.tile([P, PIECE], F32, name="first")
            vector_subtract(first[:], b, 0, neg_lse)
            store(first[:], b, 0, 1)
            middle = staging.tile([P, 2 * PIECE], F32, name="middle")
            vector_subtract(middle[:, :PIECE], b, 1, neg_lse)
            scalar_subtract(middle[:, PIECE:], b, 2, neg_lse)
            store(middle[:], b, 1, 2)
            last = staging.tile([P, PIECE], F32, name="last")
            scalar_subtract(last[:], b, 3, neg_lse)
            store(last[:], b, 3, 1)

        def finish_last_block(b, neg_lse):
            for p in range(0, PIECES, 2):
                result = staging.tile([P, 2 * PIECE], F32, name="result")
                vector_subtract(result[:, :PIECE], b, p, neg_lse)
                scalar_subtract(result[:, PIECE:], b, p + 1, neg_lse)
                store(result[:], b, p, 2)

        scores_and_sums(0)
        neg_lse_0 = neg_log_sum_exp(0)
        scores_and_sums(1)
        neg_lse_1 = neg_log_sum_exp(1)
        finish_first_block(0, neg_lse_0)
        finish_last_block(1, neg_lse_1)
